import numpy as np
import ml_dtypes


def mxq(x, axis, fmt="e4m3"):
    dtype, down = {"e4m3": (ml_dtypes.float8_e4m3fn, 7), "e5m2": (ml_dtypes.float8_e5m2, 14)}[fmt]
    v = np.moveaxis(np.asarray(x, np.float32).astype(ml_dtypes.bfloat16).astype(np.float64), axis, -1)
    blocks = v.reshape(v.shape[:-1] + (-1, 32))
    amax = np.abs(blocks).max(-1, keepdims=True)
    byte = np.maximum(np.where(amax > 0, np.frexp(amax)[1] - 1 + 127, 0) - down, 1)
    scale = np.exp2(byte - 127.0)
    codes = (blocks / scale).astype(np.float32).astype(dtype).astype(np.float64)
    return np.moveaxis((codes * scale).reshape(v.shape), -1, axis)


WIDE = False


def mx_kscale(k):
    if not WIDE:
        return np.ones(k)
    levels = np.array([10, -10, 5, -5, 0])
    if k % 512:
        return np.exp2(np.random.permutation(np.resize(levels, k // 32))).repeat(32)
    a = np.empty((k // 512, 16))
    for p in range(k // 512):
        a[p, :8] = np.random.permutation(np.resize(levels, 8))
        for g in range(8):
            far = levels[np.abs(levels - a[p, g]) >= 10]
            a[p, g + 8] = far[np.random.randint(len(far))]
    return np.exp2(a.ravel()).repeat(32)


BF16 = ml_dtypes.bfloat16


def bf(x):
    return np.asarray(x, np.float32).astype(BF16)


def f64(x):
    return np.asarray(x).astype(np.float64)


B, S_IMG, S_TXT, D, H, HD = 1, 768, 256, 1536, 12, 128
S = S_TXT + S_IMG
E = H * HD
EPS = 1e-5


def rmsnorm(x, w):
    var = np.mean(np.square(x), axis=-1, keepdims=True)
    return x * (1.0 / np.sqrt(var + EPS)) * w


def rope(x, cos, sin):
    xr = x.reshape(x.shape[:-1] + (HD // 2, 2))
    x_rot = np.stack([-xr[..., 1], xr[..., 0]], axis=-1).reshape(x.shape)
    return x * cos[None, :, None, :] + x_rot * sin[None, :, None, :]


def setup_inputs():
    r = np.random.standard_normal
    s, u = mx_kscale(D), mx_kscale(D)
    pw = 0.015 / np.sqrt(D)
    return {"hidden_states": bf(r((B, S_IMG, D)) * s),
            "encoder_hidden_states": bf(r((B, S_TXT, D)) * u),
            "rope_cos": bf(np.random.uniform(size=(S, HD))),
            "rope_sin": bf(np.random.uniform(size=(S, HD))),
            "Wq": bf(r((E, D)) * pw / s),
            "Wk": bf(r((E, D)) * pw / s),
            "Waq": bf(r((E, D)) * pw / u),
            "baq": bf(r(E) * 0.005),
            "Wak": bf(r((E, D)) * pw / u),
            "bak": bf(r(E) * 0.005),
            "wq_norm": bf(1.75 + 0.15 * r(HD)),
            "wk_norm": bf(1.75 + 0.15 * r(HD)),
            "waq_norm": bf(1.75 + 0.15 * r(HD)),
            "wak_norm": bf(1.75 + 0.15 * r(HD))}


def reference(hidden_states, encoder_hidden_states, rope_cos, rope_sin, Wq, Wk, Waq, baq, Wak, bak, wq_norm, wk_norm, waq_norm, wak_norm):
    xq = mxq(f64(hidden_states), 2, "e4m3")
    cq = mxq(f64(encoder_hidden_states), 2, "e4m3")
    q = (xq @ mxq(f64(Wq).T, 0, "e4m3")).reshape(B, S_IMG, H, HD)
    k = (xq @ mxq(f64(Wk).T, 0, "e4m3")).reshape(B, S_IMG, H, HD)
    q = rmsnorm(q, f64(wq_norm))
    k = rmsnorm(k, f64(wk_norm))
    eq = ((cq @ mxq(f64(Waq).T, 0, "e4m3")) + f64(baq)).reshape(B, S_TXT, H, HD)
    ek = ((cq @ mxq(f64(Wak).T, 0, "e4m3")) + f64(bak)).reshape(B, S_TXT, H, HD)
    eq = rmsnorm(eq, f64(waq_norm))
    ek = rmsnorm(ek, f64(wak_norm))
    q = np.concatenate([eq, q], axis=1)
    k = np.concatenate([ek, k], axis=1)
    return rope(q, f64(rope_cos), f64(rope_sin)), rope(k, f64(rope_cos), f64(rope_sin))

@@ -1,0 +1,285 @@
+from contextlib import ExitStack
+
+import concourse.mybir as mybir
+from concourse.masks import make_identity
+
+F32 = mybir.dt.float32
+BF16 = mybir.dt.bfloat16
+I32 = mybir.dt.int32
+U32 = mybir.dt.uint32
+U8 = mybir.dt.uint8
+FP8X4 = mybir.dt.float8_e4m3fn_x4
+ACT = mybir.ActivationFunctionType
+ALU = mybir.AluOpType
+
+P = 128
+D_MODEL = 1536
+WORDS = D_MODEL // 2
+K_PASS = 512
+PASSES = D_MODEL // K_PASS
+HEAD_DIM = 128
+PAIRS = HEAD_DIM // 2
+E_OUT = 1536
+CHUNK = 512
+CHUNK_HEADS = CHUNK // HEAD_DIM
+CHUNK_ROW_TILES = CHUNK // P
+CHUNKS = E_OUT // CHUNK
+TILES = 8
+TEXT_TILES = 2
+UNIT_ROW_TILES = 2
+UNIT_ROWS = UNIT_ROW_TILES * P
+EPS = 1e-5
+RAW_CHUNKS = 4
+UNITS_A_STEP_AT_FIRST = 3
+LEAD = 7
+
+FLOPS = 2 * 2 * 1024 * D_MODEL * E_OUT
+
+
+def tile_flux2attention_pa_kernel(
+    tc,
+    hidden_states,
+    encoder_hidden_states,
+    rope_cos,
+    rope_sin,
+    Wq,
+    Wk,
+    Waq,
+    baq,
+    Wak,
+    bak,
+    wq_norm,
+    wk_norm,
+    waq_norm,
+    wak_norm,
+    out_0,
+    out_1,
+):
+    nc = tc.nc
+    with ExitStack() as ctx:
+        ctx.enter_context(tc.manual_schedule())
+        const = ctx.enter_context(tc.tile_pool(name="const", bufs=1))
+        raw_pool = ctx.enter_context(tc.tile_pool(name="raw", bufs=RAW_CHUNKS))
+        grouped_pool = ctx.enter_context(tc.tile_pool(name="grouped", bufs=8))
+        quant_pool = ctx.enter_context(tc.tile_pool(name="quant", bufs=3))
+        work = ctx.enter_context(tc.tile_pool(name="work", bufs=3))
+        terms_pool = ctx.enter_context(tc.tile_pool(name="terms", bufs=5))
+        rotated_pool = ctx.enter_context(tc.tile_pool(name="rotated", bufs=6))
+        small = ctx.enter_context(tc.tile_pool(name="small", bufs=6))
+        psum_t = ctx.enter_context(tc.psum_pool(name="psum_t", bufs=4))
+        psum_acc = ctx.enter_context(tc.psum_pool(name="psum_acc", bufs=4))
+
+        x_txt = encoder_hidden_states[0].rearrange("(t p) k -> p t k", p=P)
+        x_img = hidden_states[0].rearrange("(t p) k -> p t k", p=P)
+        out_q = out_0[0].rearrange("(t p) h d -> p t (h d)", p=P)
+        out_k = out_1[0].rearrange("(t p) h d -> p t (h d)", p=P)
+
+        x_raw = const.tile([P, TILES, D_MODEL], BF16)
+        x_codes = const.tile([P, PASSES, TILES * P], U32, align_bytes=64)
+        x_scales = const.tile([P, PASSES, TILES * P], U8, align_bytes=64)
+        cos_sb = const.tile([P, TILES, PAIRS, 2], BF16)
+        sin_sb = const.tile([P, TILES, PAIRS, 2], BF16)
+        gain_rows = const.tile([P, 4 * HEAD_DIM], BF16)
+        bias_rows = const.tile([P, 2 * E_OUT], BF16)
+        gain_sb = const.tile([P, 4, HEAD_DIM], BF16)
+        bias_sb = const.tile([P, 2 * E_OUT], BF16)
+        one = const.tile([P, 1], F32)
+        unused = const.tile([P, 1], F32)
+        ones = const.tile([P, P], BF16)
+        ident = const.tile([P, P], F32)
+        rot = const.tile([P, TILES, 2, PAIRS, 2], F32)
+        factors_q = const.tile([P, TILES, HEAD_DIM, 2], F32)
+        factors_k = const.tile([P, TILES, HEAD_DIM, 2], F32)
+
+        chunks = []
+        for w_img, w_txt, bias_col, factors, out_rows in (
+            (Wq, Waq, 0, factors_q, out_q),
+            (Wk, Wak, E_OUT, factors_k, out_k),
+        ):
+            for c in range(CHUNKS):
+                chunks.append((w_img, c * CHUNK, None, factors, out_rows, range(TEXT_TILES, TILES)))
+                chunks.append((w_txt, c * CHUNK, bias_col + c * CHUNK, factors, out_rows, range(TEXT_TILES)))
+        works = [(n, t) for n in range(len(chunks)) for t in chunks[n][5]]
+
+        needs = []
+        for n, t in works:
+            for need in (("x", t // UNIT_ROW_TILES), ("w", n)):
+                if need not in needs:
+                    needs.append(need)
+        units = []
+        for kind, which in needs:
+            row_tiles = UNIT_ROW_TILES if kind == "x" else CHUNK_ROW_TILES
+            for g in range(PASSES):
+                for r in range(0, row_tiles, UNIT_ROW_TILES):
+                    units.append((kind, which, g, r))
+        units_before_the_loop = PASSES + PASSES * CHUNK_ROW_TILES // UNIT_ROW_TILES
+
+        def load_tokens(pair):
+            t0 = UNIT_ROW_TILES * pair
+            stream, first = (x_txt, t0) if t0 < TEXT_TILES else (x_img, t0 - TEXT_TILES)
+            nc.sync.dma_start(out=x_raw[:, t0 : t0 + UNIT_ROW_TILES, :], in_=stream[:, first : first + UNIT_ROW_TILES, :])
+
+        w_raw = {}
+
+        def load_chunk(n, pieces=1):
+            weight, e0 = chunks[n][0], chunks[n][1]
+            w_raw[n] = raw_pool.tile([P, CHUNK_ROW_TILES, D_MODEL], BF16, name="w_raw")
+            rows = weight[e0 : e0 + CHUNK, :].rearrange("(r p) k -> p r k", p=P)
+            for i in range(pieces):
+                k_range = slice(i * D_MODEL // pieces, (i + 1) * D_MODEL // pieces)
+                nc.sync.dma_start(out=w_raw[n][:, :, k_range], in_=rows[:, :, k_range])
+
+        nc.vector.memset(gain_rows[:].bitcast(I32), 0)
+        nc.vector.memset(bias_rows[:].bitcast(I32), 0)
+        nc.vector.memset(ones[:], 1.0)
+        nc.vector.memset(one[:], 1.0)
+        make_identity(nc, ident[:])
+
+        for i, gain in enumerate((wq_norm, wk_norm, waq_norm, wak_norm)):
+            nc.scalar.dma_start(
+                out=gain_rows[0:1, i * HEAD_DIM : (i + 1) * HEAD_DIM], in_=gain.rearrange("(o d) -> o d", o=1)
+            )
+        for table_sb, table in ((cos_sb, rope_cos), (sin_sb, rope_sin)):
+            nc.scalar.dma_start(
+                out=table_sb[:].rearrange("p t i j -> p t (i j)"), in_=table.rearrange("(t p) d -> p t d", p=P)
+            )
+        nc.scalar.activation(out=unused[:], in_=one[:], func=ACT.Abs_reciprocal_sqrt)
+        for i, bias in enumerate((baq, bak)):
+            nc.gpsimd.dma_start(
+                out=bias_rows[0:1, i * E_OUT : (i + 1) * E_OUT], in_=bias.rearrange("(o e) -> o e", o=1)
+            )
+        for kind, which in needs:
+            if kind == "x":
+                load_tokens(which)
+            elif which < RAW_CHUNKS:
+                load_chunk(which, pieces=(PASSES if which == 0 else 1))
+
+        def spread(rows, target):
+            bank = psum_acc.tile([P, CHUNK], F32, name="acc")
+            nc.tensor.matmul(out=bank[:], lhsT=ones[:], rhs=rows, start=True, stop=True)
+            nc.scalar.copy(out=target, in_=bank[:])
+
+        def spread_bias(n):
+            cols = slice(chunks[n][2], chunks[n][2] + CHUNK)
+            spread(bias_rows[:, cols], bias_sb[:, cols])
+
+        w_codes = {}
+        w_scales = {}
+
+        def transpose_unit(kind, which, g, r0, vector_copies=False):
+            if kind == "x":
+                words = x_raw[:].rearrange("p t k -> p (t k)").bitcast(F32)
+                r0 = UNIT_ROW_TILES * which
+                codes, scales = x_codes, x_scales
+            else:
+                if g == 0 and r0 == 0:
+                    w_codes[which] = quant_pool.tile([P, PASSES, CHUNK], U32, align_bytes=64, name="w_codes")
+                    w_scales[which] = quant_pool.tile([P, PASSES, CHUNK], U8, align_bytes=64, name="w_scales")
+                words = w_raw[which][:].rearrange("p r k -> p (r k)").bitcast(F32)
+                codes, scales = w_codes[which], w_scales[which]
+            xt = psum_t.tile([P, 2, UNIT_ROWS], F32, name="xt")
+            for u in range(2):
+                for r in range(UNIT_ROW_TILES):
+                    word = (r0 + r) * WORDS + (K_PASS // 2) * g
+                    nc.tensor.transpose(
+                        xt[:, u, r * P : (r + 1) * P], words[:, word + u : word + K_PASS // 2 : 2], ident[:]
+                    )
+            grouped = grouped_pool.tile([P, 4 * UNIT_ROWS], BF16, align_bytes=64, name="grouped")
+            grouped_words = grouped[:].bitcast(F32).rearrange("p (c u) -> p c u", u=2)
+            if vector_copies:
+                nc.vector.tensor_copy(out=grouped_words, in_=xt[:].rearrange("p u c -> p c u"))
+            else:
+                nc.scalar.copy(out=grouped_words, in_=xt[:].rearrange("p u c -> p c u"))
+            cols = slice(r0 * P, r0 * P + UNIT_ROWS)
+            return (grouped[:], codes[:, g, cols], scales[:, g, cols])
+
+        def quantise(grouped, codes, scales):
+            nc.vector.quantize_mx(out=codes.bitcast(FP8X4), scales=scales, in_=grouped)
+
+        def project(n, t):
+            bias_col = chunks[n][2]
+            acc = psum_acc.tile([P, CHUNK], F32, name="acc")
+            for g in range(PASSES):
+                nc.tensor.matmul_mx(
+                    out=acc[:],
+                    lhsT=x_codes[:, g, t * P : (t + 1) * P].bitcast(FP8X4),
+                    lhsT_scale=x_scales[:, g, t * P : (t + 1) * P],
+                    rhs=w_codes[n][:, g, :].bitcast(FP8X4),
+                    rhs_scale=w_scales[n][:, g, :],
+                    start=(g == 0),
+                    stop=(g == PASSES - 1),
+                )
+            x = acc
+            if bias_col is not None:
+                x = work.tile([P, CHUNK], F32, name="biased")
+                nc.vector.tensor_tensor(out=x[:], in0=acc[:], in1=bias_sb[:, bias_col : bias_col + CHUNK], op=ALU.add)
+
+            squares = work.tile([P, CHUNK], BF16, name="squares")
+            sum_sq = small.tile([P, CHUNK_HEADS], F32, name="sum_sq")
+            for h in range(CHUNK_HEADS):
+                head = slice(h * HEAD_DIM, (h + 1) * HEAD_DIM)
+                nc.scalar.activation(
+                    out=squares[:, head], in_=x[:, head], func=ACT.Square, accum_out=sum_sq[:, h : h + 1]
+                )
+            r = small.tile([P, CHUNK_HEADS], F32, name="r")
+            nc.scalar.activation(out=r[:], in_=sum_sq[:], func=ACT.Abs_reciprocal_sqrt, scale=1.0 / HEAD_DIM, bias=EPS)
+            return (n, t, x, r)
+
+        def rotate(n, t, x, r):
+            e0, factors, out_rows = chunks[n][1], chunks[n][3], chunks[n][4]
+            terms = terms_pool.tile([P, CHUNK_HEADS, PAIRS, 2, 2], F32, name="terms")
+            for h in range(CHUNK_HEADS):
+                nc.vector.scalar_tensor_tensor(
+                    out=terms[:, h].rearrange("p i j o -> p (i j) o"),
+                    in0=x[:, h * HEAD_DIM : (h + 1) * HEAD_DIM].unsqueeze(2).to_broadcast([P, HEAD_DIM, 2]),
+                    scalar=r[:, h : h + 1],
+                    in1=factors[:, t],
+                    op0=ALU.mult,
+                    op1=ALU.mult,
+                )
+            rotated = rotated_pool.tile([P, CHUNK_HEADS, PAIRS, 2], F32, name="rotated")
+            nc.gpsimd.tensor_tensor(out=rotated[:], in0=terms[:, :, :, 0, :], in1=terms[:, :, :, 1, :], op=ALU.add)
+            nc.sync.dma_start(out=out_rows[:, t, e0 : e0 + CHUNK], in_=rotated[:].rearrange("p h i o -> p (h i o)"))
+
+        nc.vector.tensor_copy(out=rot[:, :, 0, :, 0], in_=cos_sb[:, :, :, 0])
+        nc.vector.tensor_scalar_mul(out=rot[:, :, 0, :, 1], in0=sin_sb[:, :, :, 0], scalar1=-1.0)
+        nc.vector.tensor_copy(out=rot[:, :, 1, :, 0], in_=sin_sb[:, :, :, 1])
+        nc.vector.tensor_copy(out=rot[:, :, 1, :, 1], in_=cos_sb[:, :, :, 1])
+
+        def build_factors(factors, first_tile, n_tiles, gain_index):
+            tiles = slice(first_tile, first_tile + n_tiles)
+            nc.vector.tensor_tensor(
+                out=factors[:, tiles],
+                in0=rot[:, tiles].rearrange("p t o i j -> p t (i j) o"),
+                in1=gain_sb[:, gain_index : gain_index + 1, :].unsqueeze(3).to_broadcast([P, n_tiles, HEAD_DIM, 2]),
+                op=ALU.mult,
+            )
+
+        for i, unit in enumerate(units[0:PASSES]):
+            quantise(*transpose_unit(*unit, vector_copies=(i % 2 == 1)))
+        spread(gain_rows[:], gain_sb[:].rearrange("p i d -> p (i d)"))
+        for i, unit in enumerate(units[PASSES:units_before_the_loop]):
+            quantise(*transpose_unit(*unit, vector_copies=(i % 2 == 1)))
+        for i, factors in enumerate((factors_q, factors_k)):
+            build_factors(factors, TEXT_TILES, TILES - TEXT_TILES, i)
+            build_factors(factors, 0, TEXT_TILES, 2 + i)
+        spread_bias(1)
+
+        prepared = units_before_the_loop
+        multiplied = None
+        for step, (n, t) in enumerate(works):
+            if step == 0 or works[step - 1][0] != n:
+                if n + RAW_CHUNKS < len(chunks):
+                    load_chunk(n + RAW_CHUNKS)
+                if chunks[n][2] is not None and n + 2 < len(chunks):
+                    spread_bias(n + 2)
+            wanted = units_before_the_loop + min(UNITS_A_STEP_AT_FIRST * (step + 1), 3 * (step + 1 + LEAD) // 2)
+            copied = [transpose_unit(*unit) for unit in units[prepared:wanted]]
+            prepared = max(prepared, wanted)
+            before = multiplied
+            multiplied = project(n, t)
+            if before is not None:
+                rotate(*before)
+            for piece in copied:
+                quantise(*piece)
+        rotate(*multiplied)

@@ -1,3 +1,4 @@
+import math
 from contextlib import ExitStack
 
 import concourse.mybir as mybir
@@ -27,11 +28,10 @@ CHUNKS = E_OUT // CHUNK
 TILES = 8
 TEXT_TILES = 2
 UNIT_ROW_TILES = 2
-UNIT_ROWS = UNIT_ROW_TILES * P
 EPS = 1e-5
 RAW_CHUNKS = 4
-UNITS_A_STEP_AT_FIRST = 3
-LEAD = 7
+READY_STEPS = 2
+BIAS_STEPS = {1: 1, 9: 3, 17: 5, 25: 7, 33: 9, 41: 11}
 
 FLOPS = 2 * 2 * 1024 * D_MODEL * E_OUT
 
@@ -77,8 +77,8 @@ def tile_flux2attention_pa_kernel(
         x_raw = const.tile([P, TILES, D_MODEL], BF16)
         x_codes = const.tile([P, PASSES, TILES * P], U32, align_bytes=64)
         x_scales = const.tile([P, PASSES, TILES * P], U8, align_bytes=64)
-        cos_sb = const.tile([P, TILES, PAIRS, 2], BF16)
-        sin_sb = const.tile([P, TILES, PAIRS, 2], BF16)
+        cos_sb = const.tile([P, TILES, HEAD_DIM], BF16)
+        sin_sb = const.tile([P, TILES, HEAD_DIM], BF16)
         gain_rows = const.tile([P, 4 * HEAD_DIM], BF16)
         bias_rows = const.tile([P, 2 * E_OUT], BF16)
         gain_sb = const.tile([P, 4, HEAD_DIM], BF16)
@@ -87,9 +87,9 @@ def tile_flux2attention_pa_kernel(
         unused = const.tile([P, 1], F32)
         ones = const.tile([P, P], BF16)
         ident = const.tile([P, P], F32)
-        rot = const.tile([P, TILES, 2, PAIRS, 2], F32)
-        factors_q = const.tile([P, TILES, HEAD_DIM, 2], F32)
-        factors_k = const.tile([P, TILES, HEAD_DIM, 2], F32)
+        rot = const.tile([P, TILES, 2, PAIRS, 2], BF16)
+        factors_q = const.tile([P, TILES, 2, HEAD_DIM], F32)
+        factors_k = const.tile([P, TILES, 2, HEAD_DIM], F32)
 
         chunks = []
         for w_img, w_txt, bias_col, factors, out_rows in (
@@ -101,58 +101,59 @@ def tile_flux2attention_pa_kernel(
                 chunks.append((w_txt, c * CHUNK, bias_col + c * CHUNK, factors, out_rows, range(TEXT_TILES)))
         works = [(n, t) for n in range(len(chunks)) for t in chunks[n][5]]
 
+        first_tile = works[0][1]
+        first_pieces = [("w", 0, (0,)), ("w", 0, (1,)), ("x", None, (first_tile,)), ("w", 0, (2,)), ("w", 0, (3,))]
         needs = []
         for n, t in works:
-            for need in (("x", t // UNIT_ROW_TILES), ("w", n)):
-                if need not in needs:
+            pair = tuple(range(t - t % UNIT_ROW_TILES, t - t % UNIT_ROW_TILES + UNIT_ROW_TILES))
+            for need in (("x", None, pair), ("w", n, tuple(range(CHUNK_ROW_TILES)))):
+                if need[0] == "x":
+                    need = ("x", None, tuple(tile for tile in pair if tile != first_tile))
+                if need not in needs and need[1] != 0:
                     needs.append(need)
+        first_units = [piece + (g,) for piece in first_pieces for g in range(PASSES)]
         units = []
-        for kind, which in needs:
-            row_tiles = UNIT_ROW_TILES if kind == "x" else CHUNK_ROW_TILES
+        for kind, n, rows in needs:
             for g in range(PASSES):
-                for r in range(0, row_tiles, UNIT_ROW_TILES):
-                    units.append((kind, which, g, r))
-        units_before_the_loop = PASSES + PASSES * CHUNK_ROW_TILES // UNIT_ROW_TILES
-
-        def load_tokens(pair):
-            t0 = UNIT_ROW_TILES * pair
-            stream, first = (x_txt, t0) if t0 < TEXT_TILES else (x_img, t0 - TEXT_TILES)
-            nc.sync.dma_start(out=x_raw[:, t0 : t0 + UNIT_ROW_TILES, :], in_=stream[:, first : first + UNIT_ROW_TILES, :])
+                for i in range(0, len(rows), UNIT_ROW_TILES):
+                    units.append((kind, n, rows[i : i + UNIT_ROW_TILES], g))
 
         w_raw = {}
 
-        def load_chunk(n, pieces=1):
+        def load_rows(kind, n, rows):
+            first, last = rows[0], rows[-1] + 1
+            if kind == "x":
+                stream, skip = (x_txt, 0) if first < TEXT_TILES else (x_img, TEXT_TILES)
+                nc.sync.dma_start(out=x_raw[:, first:last, :], in_=stream[:, first - skip : last - skip, :])
+                return
             weight, e0 = chunks[n][0], chunks[n][1]
-            w_raw[n] = raw_pool.tile([P, CHUNK_ROW_TILES, D_MODEL], BF16, name="w_raw")
-            rows = weight[e0 : e0 + CHUNK, :].rearrange("(r p) k -> p r k", p=P)
-            for i in range(pieces):
-                k_range = slice(i * D_MODEL // pieces, (i + 1) * D_MODEL // pieces)
-                nc.sync.dma_start(out=w_raw[n][:, :, k_range], in_=rows[:, :, k_range])
+            if n not in w_raw:
+                w_raw[n] = raw_pool.tile([P, CHUNK_ROW_TILES, D_MODEL], BF16, name="w_raw")
+            chunk_rows = weight[e0 : e0 + CHUNK, :].rearrange("(r p) k -> p r k", p=P)
+            nc.sync.dma_start(out=w_raw[n][:, first:last, :], in_=chunk_rows[:, first:last, :])
 
         nc.vector.memset(gain_rows[:].bitcast(I32), 0)
-        nc.vector.memset(bias_rows[:].bitcast(I32), 0)
         nc.vector.memset(ones[:], 1.0)
         nc.vector.memset(one[:], 1.0)
         make_identity(nc, ident[:])
+        nc.gpsimd.memset(bias_rows[:].bitcast(I32), 0)
 
         for i, gain in enumerate((wq_norm, wk_norm, waq_norm, wak_norm)):
             nc.scalar.dma_start(
                 out=gain_rows[0:1, i * HEAD_DIM : (i + 1) * HEAD_DIM], in_=gain.rearrange("(o d) -> o d", o=1)
-            )
-        for table_sb, table in ((cos_sb, rope_cos), (sin_sb, rope_sin)):
-            nc.scalar.dma_start(
-                out=table_sb[:].rearrange("p t i j -> p t (i j)"), in_=table.rearrange("(t p) d -> p t d", p=P)
             )
         nc.scalar.activation(out=unused[:], in_=one[:], func=ACT.Abs_reciprocal_sqrt)
         for i, bias in enumerate((baq, bak)):
             nc.gpsimd.dma_start(
                 out=bias_rows[0:1, i * E_OUT : (i + 1) * E_OUT], in_=bias.rearrange("(o e) -> o e", o=1)
             )
-        for kind, which in needs:
-            if kind == "x":
-                load_tokens(which)
-            elif which < RAW_CHUNKS:
-                load_chunk(which, pieces=(PASSES if which == 0 else 1))
+        for piece in first_pieces:
+            load_rows(*piece)
+        for table_sb, table in ((cos_sb, rope_cos), (sin_sb, rope_sin)):
+            nc.sync.dma_start(out=table_sb[:], in_=table.rearrange("(t p) d -> p t d", p=P))
+        for kind, n, rows in needs:
+            if kind == "x" or n < RAW_CHUNKS:
+                load_rows(kind, n, rows)
 
         def spread(rows, target):
             bank = psum_acc.tile([P, CHUNK], F32, name="acc")
@@ -166,42 +167,41 @@ def tile_flux2attention_pa_kernel(
         w_codes = {}
         w_scales = {}
 
-        def transpose_unit(kind, which, g, r0, vector_copies=False):
+        def transpose_unit(kind, n, rows, g, vector_copies=False):
             if kind == "x":
                 words = x_raw[:].rearrange("p t k -> p (t k)").bitcast(F32)
-                r0 = UNIT_ROW_TILES * which
                 codes, scales = x_codes, x_scales
             else:
-                if g == 0 and r0 == 0:
-                    w_codes[which] = quant_pool.tile([P, PASSES, CHUNK], U32, align_bytes=64, name="w_codes")
-                    w_scales[which] = quant_pool.tile([P, PASSES, CHUNK], U8, align_bytes=64, name="w_scales")
-                words = w_raw[which][:].rearrange("p r k -> p (r k)").bitcast(F32)
-                codes, scales = w_codes[which], w_scales[which]
-            xt = psum_t.tile([P, 2, UNIT_ROWS], F32, name="xt")
+                if n not in w_codes:
+                    w_codes[n] = quant_pool.tile([P, PASSES, CHUNK], U32, align_bytes=64, name="w_codes")
+                    w_scales[n] = quant_pool.tile([P, PASSES, CHUNK], U8, align_bytes=64, name="w_scales")
+                words = w_raw[n][:].rearrange("p r k -> p (r k)").bitcast(F32)
+                codes, scales = w_codes[n], w_scales[n]
+            n_rows = P * len(rows)
+            xt = psum_t.tile([P, 2, n_rows], F32, name="xt")
             for u in range(2):
-                for r in range(UNIT_ROW_TILES):
-                    word = (r0 + r) * WORDS + (K_PASS // 2) * g
+                for i, row_tile in enumerate(rows):
+                    word = row_tile * WORDS + (K_PASS // 2) * g
                     nc.tensor.transpose(
-                        xt[:, u, r * P : (r + 1) * P], words[:, word + u : word + K_PASS // 2 : 2], ident[:]
+                        xt[:, u, i * P : (i + 1) * P], words[:, word + u : word + K_PASS // 2 : 2], ident[:]
                     )
-            grouped = grouped_pool.tile([P, 4 * UNIT_ROWS], BF16, align_bytes=64, name="grouped")
+            grouped = grouped_pool.tile([P, 4 * n_rows], BF16, align_bytes=64, name="grouped")
             grouped_words = grouped[:].bitcast(F32).rearrange("p (c u) -> p c u", u=2)
             if vector_copies:
                 nc.vector.tensor_copy(out=grouped_words, in_=xt[:].rearrange("p u c -> p c u"))
             else:
                 nc.scalar.copy(out=grouped_words, in_=xt[:].rearrange("p u c -> p c u"))
-            cols = slice(r0 * P, r0 * P + UNIT_ROWS)
+            cols = slice(rows[0] * P, rows[0] * P + n_rows)
             return (grouped[:], codes[:, g, cols], scales[:, g, cols])
 
         def quantise(grouped, codes, scales):
             nc.vector.quantize_mx(out=codes.bitcast(FP8X4), scales=scales, in_=grouped)
 
-        def project(n, t):
-            bias_col = chunks[n][2]
-            acc = psum_acc.tile([P, CHUNK], F32, name="acc")
+        def multiply(n, t, state):
+            state["acc"] = psum_acc.tile([P, CHUNK], F32, name="acc")
             for g in range(PASSES):
                 nc.tensor.matmul_mx(
-                    out=acc[:],
+                    out=state["acc"][:],
                     lhsT=x_codes[:, g, t * P : (t + 1) * P].bitcast(FP8X4),
                     lhsT_scale=x_scales[:, g, t * P : (t + 1) * P],
                     rhs=w_codes[n][:, g, :].bitcast(FP8X4),
@@ -209,11 +209,18 @@ def tile_flux2attention_pa_kernel(
                     start=(g == 0),
                     stop=(g == PASSES - 1),
                 )
-            x = acc
-            if bias_col is not None:
-                x = work.tile([P, CHUNK], F32, name="biased")
-                nc.vector.tensor_tensor(out=x[:], in0=acc[:], in1=bias_sb[:, bias_col : bias_col + CHUNK], op=ALU.add)
 
+        def add_bias(n, t, state):
+            bias_col = chunks[n][2]
+            state["x"] = state["acc"]
+            if bias_col is not None:
+                state["x"] = work.tile([P, CHUNK], F32, name="biased")
+                nc.vector.tensor_tensor(
+                    out=state["x"][:], in0=state["acc"][:], in1=bias_sb[:, bias_col : bias_col + CHUNK], op=ALU.add
+                )
+
+        def norm(n, t, state):
+            x = state["x"]
             squares = work.tile([P, CHUNK], BF16, name="squares")
             sum_sq = small.tile([P, CHUNK_HEADS], F32, name="sum_sq")
             for h in range(CHUNK_HEADS):
@@ -221,65 +228,127 @@ def tile_flux2attention_pa_kernel(
                 nc.scalar.activation(
                     out=squares[:, head], in_=x[:, head], func=ACT.Square, accum_out=sum_sq[:, h : h + 1]
                 )
-            r = small.tile([P, CHUNK_HEADS], F32, name="r")
-            nc.scalar.activation(out=r[:], in_=sum_sq[:], func=ACT.Abs_reciprocal_sqrt, scale=1.0 / HEAD_DIM, bias=EPS)
-            return (n, t, x, r)
+            state["r"] = small.tile([P, CHUNK_HEADS], F32, name="r")
+            nc.scalar.activation(
+                out=state["r"][:], in_=sum_sq[:], func=ACT.Abs_reciprocal_sqrt, scale=1.0 / HEAD_DIM, bias=EPS
+            )
 
-        def rotate(n, t, x, r):
-            e0, factors, out_rows = chunks[n][1], chunks[n][3], chunks[n][4]
-            terms = terms_pool.tile([P, CHUNK_HEADS, PAIRS, 2, 2], F32, name="terms")
+        def rotate(n, t, state):
+            factors = chunks[n][3]
+            x, r = state["x"], state["r"]
+            state["terms"] = terms_pool.tile([P, CHUNK_HEADS, 2, HEAD_DIM], F32, name="terms")
             for h in range(CHUNK_HEADS):
                 nc.vector.scalar_tensor_tensor(
-                    out=terms[:, h].rearrange("p i j o -> p (i j) o"),
-                    in0=x[:, h * HEAD_DIM : (h + 1) * HEAD_DIM].unsqueeze(2).to_broadcast([P, HEAD_DIM, 2]),
+                    out=state["terms"][:, h],
+                    in0=x[:, h * HEAD_DIM : (h + 1) * HEAD_DIM].unsqueeze(1).to_broadcast([P, 2, HEAD_DIM]),
                     scalar=r[:, h : h + 1],
                     in1=factors[:, t],
                     op0=ALU.mult,
                     op1=ALU.mult,
                 )
+
+        def add_and_store(n, t, state):
+            e0, out_rows = chunks[n][1], chunks[n][4]
+            terms = state["terms"][:].rearrange("p h o (i j) -> p h i o j", j=2)
             rotated = rotated_pool.tile([P, CHUNK_HEADS, PAIRS, 2], F32, name="rotated")
-            nc.gpsimd.tensor_tensor(out=rotated[:], in0=terms[:, :, :, 0, :], in1=terms[:, :, :, 1, :], op=ALU.add)
+            nc.gpsimd.tensor_tensor(
+                out=rotated[:],
+                in0=terms[:, :, :, :, 0],
+                in1=terms[:, :, :, :, 1],
+                op=ALU.add,
+            )
             nc.sync.dma_start(out=out_rows[:, t, e0 : e0 + CHUNK], in_=rotated[:].rearrange("p h i o -> p (h i o)"))
 
-        nc.vector.tensor_copy(out=rot[:, :, 0, :, 0], in_=cos_sb[:, :, :, 0])
-        nc.vector.tensor_scalar_mul(out=rot[:, :, 0, :, 1], in0=sin_sb[:, :, :, 0], scalar1=-1.0)
-        nc.vector.tensor_copy(out=rot[:, :, 1, :, 0], in_=sin_sb[:, :, :, 1])
-        nc.vector.tensor_copy(out=rot[:, :, 1, :, 1], in_=cos_sb[:, :, :, 1])
-
-        def build_factors(factors, first_tile, n_tiles, gain_index):
+        def build_rot(first_tile, n_tiles):
             tiles = slice(first_tile, first_tile + n_tiles)
-            nc.vector.tensor_tensor(
+            cos = cos_sb[:, tiles].rearrange("p t (i o) -> p t i o", o=2)
+            sin = sin_sb[:, tiles].rearrange("p t (i o) -> p t i o", o=2)
+            nc.vector.tensor_copy(out=rot[:, tiles, 0, :, 0], in_=cos[:, :, :, 0])
+            nc.vector.tensor_scalar_mul(out=rot[:, tiles, 0, :, 1], in0=sin[:, :, :, 0], scalar1=-1.0)
+            nc.vector.tensor_copy(out=rot[:, tiles, 1, :, 0], in_=sin[:, :, :, 1])
+            nc.vector.tensor_copy(out=rot[:, tiles, 1, :, 1], in_=cos[:, :, :, 1])
+
+        def build_factors(factors, first_tile, n_tiles, gain_index, engine):
+            tiles = slice(first_tile, first_tile + n_tiles)
+            engine.tensor_tensor(
                 out=factors[:, tiles],
-                in0=rot[:, tiles].rearrange("p t o i j -> p t (i j) o"),
-                in1=gain_sb[:, gain_index : gain_index + 1, :].unsqueeze(3).to_broadcast([P, n_tiles, HEAD_DIM, 2]),
+                in0=rot[:, tiles].rearrange("p t o i j -> p t o (i j)"),
+                in1=gain_sb[:, gain_index : gain_index + 1, :].unsqueeze(1).to_broadcast([P, n_tiles, 2, HEAD_DIM]),
                 op=ALU.mult,
             )
 
-        for i, unit in enumerate(units[0:PASSES]):
-            quantise(*transpose_unit(*unit, vector_copies=(i % 2 == 1)))
+        for unit in first_units:
+            quantise(*transpose_unit(*unit))
         spread(gain_rows[:], gain_sb[:].rearrange("p i d -> p (i d)"))
-        for i, unit in enumerate(units[PASSES:units_before_the_loop]):
-            quantise(*transpose_unit(*unit, vector_copies=(i % 2 == 1)))
-        for i, factors in enumerate((factors_q, factors_k)):
-            build_factors(factors, TEXT_TILES, TILES - TEXT_TILES, i)
-            build_factors(factors, 0, TEXT_TILES, 2 + i)
-        spread_bias(1)
+        build_rot(TEXT_TILES, TILES - TEXT_TILES)
+        build_factors(factors_q, TEXT_TILES, 1, 0, nc.vector)
 
-        prepared = units_before_the_loop
-        multiplied = None
-        for step, (n, t) in enumerate(works):
+        due = []
+        for step in range(len(works)):
+            tiles_and_chunks = works[: step + 1 + READY_STEPS]
+            due.append(
+                sum(
+                    any((kind == "w" and n == unit_n) or (kind == "x" and t in rows) for n, t in tiles_and_chunks)
+                    for kind, unit_n, rows, g in units
+                )
+            )
+
+        def pace(step):
+            known = [(-1, 0)] + list(enumerate(due))
+            hull = max(
+                ya + (yb - ya) * (step - a) / (b - a) for a, ya in known for b, yb in known if a < step <= b
+            )
+            return math.ceil(hull - 1e-9)
+
+        prepared = 0
+        states = {}
+        to_quantise = {}
+        last = len(works) - 1
+
+        def at(stage, s):
+            if 0 <= s <= last:
+                stage(works[s][0], works[s][1], states[s])
+
+        def start_chunk(step):
+            n, t = works[step]
             if step == 0 or works[step - 1][0] != n:
                 if n + RAW_CHUNKS < len(chunks):
-                    load_chunk(n + RAW_CHUNKS)
-                if chunks[n][2] is not None and n + 2 < len(chunks):
-                    spread_bias(n + 2)
-            wanted = units_before_the_loop + min(UNITS_A_STEP_AT_FIRST * (step + 1), 3 * (step + 1 + LEAD) // 2)
-            copied = [transpose_unit(*unit) for unit in units[prepared:wanted]]
-            prepared = max(prepared, wanted)
-            before = multiplied
-            multiplied = project(n, t)
-            if before is not None:
-                rotate(*before)
-            for piece in copied:
+                    load_rows("w", n + RAW_CHUNKS, tuple(range(CHUNK_ROW_TILES)))
+            if step in BIAS_STEPS:
+                spread_bias(BIAS_STEPS[step])
+
+        done = [0]
+
+        def prepare(step):
+            if step <= last:
+                wanted = max(done[0], pace(step))
+                to_quantise[step] = [transpose_unit(*unit) for unit in units[done[0] : wanted]]
+                done[0] = wanted
+
+        def finish(step):
+            for piece in to_quantise.pop(step, ()):
                 quantise(*piece)
-        rotate(*multiplied)
+
+        def tables(step):
+            if step + TEXT_TILES + 1 < TILES:
+                build_factors(factors_q, step + TEXT_TILES + 1, 1, 0, nc.vector)
+            if step == 2:
+                build_rot(0, TEXT_TILES)
+                build_factors(factors_q, 0, TEXT_TILES, 2, nc.vector)
+            if step == 12:
+                build_factors(factors_k, TEXT_TILES, TILES - TEXT_TILES, 1, nc.vector)
+            if step == 16:
+                build_factors(factors_k, 0, TEXT_TILES, 3, nc.vector)
+
+        for step in range(len(works) + 1):
+            if step <= last:
+                states[step] = {}
+                start_chunk(step)
+            prepare(step)
+            at(multiply, step)
+            at(add_bias, step)
+            at(norm, step)
+            at(rotate, step - 1)
+            at(add_and_store, step - 1)
+            finish(step)
+            tables(step)

@@ -31,6 +31,7 @@ UNIT_ROW_TILES = 2
 EPS = 1e-5
 RAW_CHUNKS = 4
 READY_STEPS = 2
+PARK_K_STEP = 27
 BIAS_STEPS = {1: 1, 9: 3, 17: 5, 25: 7, 33: 9, 41: 11}
 
 FLOPS = 2 * 2 * 1024 * D_MODEL * E_OUT
@@ -66,8 +67,9 @@ def tile_flux2attention_pa_kernel(
         terms_pool = ctx.enter_context(tc.tile_pool(name="terms", bufs=5))
         rotated_pool = ctx.enter_context(tc.tile_pool(name="rotated", bufs=6))
         small = ctx.enter_context(tc.tile_pool(name="small", bufs=6))
-        psum_t = ctx.enter_context(tc.psum_pool(name="psum_t", bufs=4))
+        psum_t = ctx.enter_context(tc.psum_pool(name="psum_t", bufs=3))
         psum_acc = ctx.enter_context(tc.psum_pool(name="psum_acc", bufs=4))
+        psum_f = ctx.enter_context(tc.psum_pool(name="psum_f", bufs=1))
 
         x_txt = encoder_hidden_states[0].rearrange("(t p) k -> p t k", p=P)
         x_img = hidden_states[0].rearrange("(t p) k -> p t k", p=P)
@@ -87,9 +89,9 @@ def tile_flux2attention_pa_kernel(
         unused = const.tile([P, 1], F32)
         ones = const.tile([P, P], BF16)
         ident = const.tile([P, P], F32)
-        rot = const.tile([P, TILES, 2, PAIRS, 2], BF16)
-        factors_q = const.tile([P, TILES, 2, HEAD_DIM], F32)
-        factors_k = const.tile([P, TILES, 2, HEAD_DIM], F32)
+        rot = const.tile([P, TILES, PAIRS, 2, 2], BF16)
+        factors_q = {"sbuf": const.tile([P, TILES, HEAD_DIM, 2], F32, name="factors_q")}
+        factors_k = {"sbuf": const.tile([P, TILES, HEAD_DIM, 2], F32, name="factors_k")}
 
         chunks = []
         for w_img, w_txt, bias_col, factors, out_rows in (
@@ -236,25 +238,25 @@ def tile_flux2attention_pa_kernel(
         def rotate(n, t, state):
             factors = chunks[n][3]
             x, r = state["x"], state["r"]
-            state["terms"] = terms_pool.tile([P, CHUNK_HEADS, 2, HEAD_DIM], F32, name="terms")
+            state["terms"] = terms_pool.tile([P, CHUNK_HEADS, PAIRS, 2, 2], F32, name="terms")
             for h in range(CHUNK_HEADS):
                 nc.vector.scalar_tensor_tensor(
-                    out=state["terms"][:, h],
-                    in0=x[:, h * HEAD_DIM : (h + 1) * HEAD_DIM].unsqueeze(1).to_broadcast([P, 2, HEAD_DIM]),
+                    out=state["terms"][:, h].rearrange("p i j o -> p (i j) o"),
+                    in0=x[:, h * HEAD_DIM : (h + 1) * HEAD_DIM].unsqueeze(2).to_broadcast([P, HEAD_DIM, 2]),
                     scalar=r[:, h : h + 1],
-                    in1=factors[:, t],
+                    in1=factors["text" if t < TEXT_TILES else "sbuf"][:, t],
                     op0=ALU.mult,
                     op1=ALU.mult,
                 )
 
         def add_and_store(n, t, state):
             e0, out_rows = chunks[n][1], chunks[n][4]
-            terms = state["terms"][:].rearrange("p h o (i j) -> p h i o j", j=2)
+            terms = state["terms"]
             rotated = rotated_pool.tile([P, CHUNK_HEADS, PAIRS, 2], F32, name="rotated")
             nc.gpsimd.tensor_tensor(
                 out=rotated[:],
-                in0=terms[:, :, :, :, 0],
-                in1=terms[:, :, :, :, 1],
+                in0=terms[:, :, :, 0, :],
+                in1=terms[:, :, :, 1, :],
                 op=ALU.add,
             )
             nc.sync.dma_start(out=out_rows[:, t, e0 : e0 + CHUNK], in_=rotated[:].rearrange("p h i o -> p (h i o)"))
@@ -263,18 +265,28 @@ def tile_flux2attention_pa_kernel(
             tiles = slice(first_tile, first_tile + n_tiles)
             cos = cos_sb[:, tiles].rearrange("p t (i o) -> p t i o", o=2)
             sin = sin_sb[:, tiles].rearrange("p t (i o) -> p t i o", o=2)
-            nc.vector.tensor_copy(out=rot[:, tiles, 0, :, 0], in_=cos[:, :, :, 0])
-            nc.vector.tensor_scalar_mul(out=rot[:, tiles, 0, :, 1], in0=sin[:, :, :, 0], scalar1=-1.0)
-            nc.vector.tensor_copy(out=rot[:, tiles, 1, :, 0], in_=sin[:, :, :, 1])
-            nc.vector.tensor_copy(out=rot[:, tiles, 1, :, 1], in_=cos[:, :, :, 1])
+            nc.vector.tensor_copy(out=rot[:, tiles, :, 0, 0], in_=cos[:, :, :, 0])
+            nc.vector.tensor_scalar_mul(out=rot[:, tiles, :, 1, 0], in0=sin[:, :, :, 0], scalar1=-1.0)
+            nc.vector.tensor_copy(out=rot[:, tiles, :, 0, 1], in_=sin[:, :, :, 1])
+            nc.vector.tensor_copy(out=rot[:, tiles, :, 1, 1], in_=cos[:, :, :, 1])
 
         def build_factors(factors, first_tile, n_tiles, gain_index, engine):
             tiles = slice(first_tile, first_tile + n_tiles)
             engine.tensor_tensor(
-                out=factors[:, tiles],
-                in0=rot[:, tiles].rearrange("p t o i j -> p t o (i j)"),
-                in1=gain_sb[:, gain_index : gain_index + 1, :].unsqueeze(1).to_broadcast([P, n_tiles, 2, HEAD_DIM]),
+                out=factors["sbuf"][:, tiles],
+                in0=rot[:, tiles].rearrange("p t i j o -> p t (i j) o"),
+                in1=gain_sb[:, gain_index : gain_index + 1, :].unsqueeze(3).to_broadcast([P, n_tiles, HEAD_DIM, 2]),
                 op=ALU.mult,
+            )
+
+        def park_text_factors(factors):
+            factors["text"] = psum_f.tile([P, TEXT_TILES, HEAD_DIM, 2], F32, name="text_factors")
+            nc.tensor.matmul(
+                out=factors["text"][:].rearrange("p t d o -> p (t d o)"),
+                lhsT=ident[:],
+                rhs=factors["sbuf"][:, 0:TEXT_TILES].rearrange("p t d o -> p (t d o)"),
+                start=True,
+                stop=True,
             )
 
         for unit in first_units:
@@ -339,6 +351,10 @@ def tile_flux2attention_pa_kernel(
                 build_factors(factors_k, TEXT_TILES, TILES - TEXT_TILES, 1, nc.vector)
             if step == 16:
                 build_factors(factors_k, 0, TEXT_TILES, 3, nc.vector)
+            if step == 5:
+                park_text_factors(factors_q)
+            if step == PARK_K_STEP:
+                park_text_factors(factors_k)
 
         for step in range(len(works) + 1):
             if step <= last:

@@ -31,8 +31,7 @@ UNIT_ROW_TILES = 2
 EPS = 1e-5
 RAW_CHUNKS = 4
 READY_STEPS = 2
-PARK_K_STEP = 27
-BIAS_STEPS = {1: 1, 9: 3, 17: 5, 25: 7, 33: 9, 41: 11}
+PARK_K_STEP = 31
 
 FLOPS = 2 * 2 * 1024 * D_MODEL * E_OUT
 
@@ -82,7 +81,6 @@ def tile_flux2attention_pa_kernel(
         cos_sb = const.tile([P, TILES, HEAD_DIM], BF16)
         sin_sb = const.tile([P, TILES, HEAD_DIM], BF16)
         gain_rows = const.tile([P, 4 * HEAD_DIM], BF16)
-        bias_rows = const.tile([P, 2 * E_OUT], BF16)
         gain_sb = const.tile([P, 4, HEAD_DIM], BF16)
         bias_sb = const.tile([P, 2 * E_OUT], BF16)
         one = const.tile([P, 1], F32)
@@ -93,14 +91,19 @@ def tile_flux2attention_pa_kernel(
         factors_q = {"sbuf": const.tile([P, TILES, HEAD_DIM, 2], F32, name="factors_q")}
         factors_k = {"sbuf": const.tile([P, TILES, HEAD_DIM, 2], F32, name="factors_k")}
 
-        chunks = []
+        image_chunks, text_chunks, chunks = [], [], []
         for w_img, w_txt, bias_col, factors, out_rows in (
             (Wq, Waq, 0, factors_q, out_q),
             (Wk, Wak, E_OUT, factors_k, out_k),
         ):
             for c in range(CHUNKS):
-                chunks.append((w_img, c * CHUNK, None, factors, out_rows, range(TEXT_TILES, TILES)))
-                chunks.append((w_txt, c * CHUNK, bias_col + c * CHUNK, factors, out_rows, range(TEXT_TILES)))
+                image_chunks.append((w_img, c * CHUNK, None, factors, out_rows, range(TEXT_TILES, TILES)))
+                text_chunks.append((w_txt, c * CHUNK, bias_col + c * CHUNK, factors, out_rows, range(TEXT_TILES)))
+        for i in range(2 * CHUNKS):
+            chunks.append(image_chunks[i])
+            if i > 0:
+                chunks.append(text_chunks[i - 1])
+        chunks.append(text_chunks[-1])
         works = [(n, t) for n in range(len(chunks)) for t in chunks[n][5]]
 
         first_tile = works[0][1]
@@ -138,17 +141,12 @@ def tile_flux2attention_pa_kernel(
         nc.vector.memset(ones[:], 1.0)
         nc.vector.memset(one[:], 1.0)
         make_identity(nc, ident[:])
-        nc.gpsimd.memset(bias_rows[:].bitcast(I32), 0)
 
         for i, gain in enumerate((wq_norm, wk_norm, waq_norm, wak_norm)):
             nc.scalar.dma_start(
                 out=gain_rows[0:1, i * HEAD_DIM : (i + 1) * HEAD_DIM], in_=gain.rearrange("(o d) -> o d", o=1)
             )
         nc.scalar.activation(out=unused[:], in_=one[:], func=ACT.Abs_reciprocal_sqrt)
-        for i, bias in enumerate((baq, bak)):
-            nc.gpsimd.dma_start(
-                out=bias_rows[0:1, i * E_OUT : (i + 1) * E_OUT], in_=bias.rearrange("(o e) -> o e", o=1)
-            )
         for piece in first_pieces:
             load_rows(*piece)
         for table_sb, table in ((cos_sb, rope_cos), (sin_sb, rope_sin)):
@@ -156,15 +154,13 @@ def tile_flux2attention_pa_kernel(
         for kind, n, rows in needs:
             if kind == "x" or n < RAW_CHUNKS:
                 load_rows(kind, n, rows)
+        for i, bias in enumerate((baq, bak)):
+            nc.sync.dma_start(out=bias_sb[:, i * E_OUT : (i + 1) * E_OUT], in_=bias.partition_broadcast(P))
 
         def spread(rows, target):
             bank = psum_acc.tile([P, CHUNK], F32, name="acc")
             nc.tensor.matmul(out=bank[:], lhsT=ones[:], rhs=rows, start=True, stop=True)
             nc.scalar.copy(out=target, in_=bank[:])
-
-        def spread_bias(n):
-            cols = slice(chunks[n][2], chunks[n][2] + CHUNK)
-            spread(bias_rows[:, cols], bias_sb[:, cols])
 
         w_codes = {}
         w_scales = {}
@@ -326,8 +322,6 @@ def tile_flux2attention_pa_kernel(
             if step == 0 or works[step - 1][0] != n:
                 if n + RAW_CHUNKS < len(chunks):
                     load_rows("w", n + RAW_CHUNKS, tuple(range(CHUNK_ROW_TILES)))
-            if step in BIAS_STEPS:
-                spread_bias(BIAS_STEPS[step])
 
         done = [0]
 
@@ -347,10 +341,10 @@ def tile_flux2attention_pa_kernel(
             if step == 2:
                 build_rot(0, TEXT_TILES)
                 build_factors(factors_q, 0, TEXT_TILES, 2, nc.vector)
-            if step == 12:
-                build_factors(factors_k, TEXT_TILES, TILES - TEXT_TILES, 1, nc.vector)
-            if step == 16:
-                build_factors(factors_k, 0, TEXT_TILES, 3, nc.vector)
+            if step in (4, 5, 6):
+                build_factors(factors_k, 2 * step - 6, 2, 1, nc.gpsimd)
+            if step == 7:
+                build_factors(factors_k, 0, TEXT_TILES, 3, nc.gpsimd)
             if step == 5:
                 park_text_factors(factors_q)
             if step == PARK_K_STEP:

@@ -31,6 +31,9 @@ UNIT_ROW_TILES = 2
 EPS = 1e-5
 RAW_CHUNKS = 4
 READY_STEPS = 2
+READY_FIRST = 1
+FIRST_STEPS = 2
+UNITS_IN_A_RUN = 2
 PARK_K_STEP = 31
 
 FLOPS = 2 * 2 * 1024 * D_MODEL * E_OUT
@@ -143,15 +146,16 @@ def tile_flux2attention_pa_kernel(
         make_identity(nc, ident[:])
 
         for i, gain in enumerate((wq_norm, wk_norm, waq_norm, wak_norm)):
-            nc.scalar.dma_start(
+            nc.gpsimd.dma_start(
                 out=gain_rows[0:1, i * HEAD_DIM : (i + 1) * HEAD_DIM], in_=gain.rearrange("(o d) -> o d", o=1)
             )
         nc.scalar.activation(out=unused[:], in_=one[:], func=ACT.Abs_reciprocal_sqrt)
         for piece in first_pieces:
             load_rows(*piece)
-        for table_sb, table in ((cos_sb, rope_cos), (sin_sb, rope_sin)):
-            nc.sync.dma_start(out=table_sb[:], in_=table.rearrange("(t p) d -> p t d", p=P))
-        for kind, n, rows in needs:
+        for i, (kind, n, rows) in enumerate(needs):
+            if i == 1:
+                for table_sb, table in ((cos_sb, rope_cos), (sin_sb, rope_sin)):
+                    nc.sync.dma_start(out=table_sb[:], in_=table.rearrange("(t p) d -> p t d", p=P))
             if kind == "x" or n < RAW_CHUNKS:
                 load_rows(kind, n, rows)
         for i, bias in enumerate((baq, bak)):
@@ -293,7 +297,8 @@ def tile_flux2attention_pa_kernel(
 
         due = []
         for step in range(len(works)):
-            tiles_and_chunks = works[: step + 1 + READY_STEPS]
+            ready = READY_FIRST if step < FIRST_STEPS else READY_STEPS
+            tiles_and_chunks = works[: step + 1 + ready]
             due.append(
                 sum(
                     any((kind == "w" and n == unit_n) or (kind == "x" and t in rows) for n, t in tiles_and_chunks)
@@ -306,7 +311,7 @@ def tile_flux2attention_pa_kernel(
             hull = max(
                 ya + (yb - ya) * (step - a) / (b - a) for a, ya in known for b, yb in known if a < step <= b
             )
-            return math.ceil(hull - 1e-9)
+            return UNITS_IN_A_RUN * math.ceil((hull - 1e-9) / UNITS_IN_A_RUN)
 
         prepared = 0
         states = {}

@@ -33,7 +33,7 @@ RAW_CHUNKS = 4
 READY_STEPS = 2
 READY_FIRST = 1
 FIRST_STEPS = 2
-UNITS_IN_A_RUN = 2
+UNITS_IN_A_RUN = 1
 PARK_K_STEP = 31
 
 FLOPS = 2 * 2 * 1024 * D_MODEL * E_OUT
@@ -146,7 +146,7 @@ def tile_flux2attention_pa_kernel(
         make_identity(nc, ident[:])
 
         for i, gain in enumerate((wq_norm, wk_norm, waq_norm, wak_norm)):
-            nc.gpsimd.dma_start(
+            nc.scalar.dma_start(
                 out=gain_rows[0:1, i * HEAD_DIM : (i + 1) * HEAD_DIM], in_=gain.rearrange("(o d) -> o d", o=1)
             )
         nc.scalar.activation(out=unused[:], in_=one[:], func=ACT.Abs_reciprocal_sqrt)

@@ -34,7 +34,7 @@ READY_STEPS = 2
 READY_FIRST = 1
 FIRST_STEPS = 2
 UNITS_IN_A_RUN = 1
-PARK_K_STEP = 31
+PARK_K_STEP = 33
 
 FLOPS = 2 * 2 * 1024 * D_MODEL * E_OUT
 
@@ -224,15 +224,16 @@ def tile_flux2attention_pa_kernel(
         def norm(n, t, state):
             x = state["x"]
             squares = work.tile([P, CHUNK], BF16, name="squares")
-            sum_sq = small.tile([P, CHUNK_HEADS], F32, name="sum_sq")
+            state["sum_sq"] = small.tile([P, CHUNK_HEADS], F32, name="sum_sq")
             for h in range(CHUNK_HEADS):
                 head = slice(h * HEAD_DIM, (h + 1) * HEAD_DIM)
                 nc.scalar.activation(
-                    out=squares[:, head], in_=x[:, head], func=ACT.Square, accum_out=sum_sq[:, h : h + 1]
+                    out=squares[:, head], in_=x[:, head], func=ACT.Square, accum_out=state["sum_sq"][:, h : h + 1]
                 )
+        def norm_end(n, t, state):
             state["r"] = small.tile([P, CHUNK_HEADS], F32, name="r")
             nc.scalar.activation(
-                out=state["r"][:], in_=sum_sq[:], func=ACT.Abs_reciprocal_sqrt, scale=1.0 / HEAD_DIM, bias=EPS
+                out=state["r"][:], in_=state["sum_sq"][:], func=ACT.Abs_reciprocal_sqrt, scale=1.0 / HEAD_DIM, bias=EPS
             )
 
         def rotate(n, t, state):
@@ -253,13 +254,15 @@ def tile_flux2attention_pa_kernel(
             e0, out_rows = chunks[n][1], chunks[n][4]
             terms = state["terms"]
             rotated = rotated_pool.tile([P, CHUNK_HEADS, PAIRS, 2], F32, name="rotated")
-            nc.gpsimd.tensor_tensor(
-                out=rotated[:],
-                in0=terms[:, :, :, 0, :],
-                in1=terms[:, :, :, 1, :],
-                op=ALU.add,
-            )
-            nc.sync.dma_start(out=out_rows[:, t, e0 : e0 + CHUNK], in_=rotated[:].rearrange("p h i o -> p (h i o)"))
+            halves = ((nc.gpsimd, 0, CHUNK_HEADS // 2), (nc.vector, CHUNK_HEADS // 2, CHUNK_HEADS))
+            for engine, h0, h1 in halves if (n, t) == works[-1] else ((nc.gpsimd, 0, CHUNK_HEADS),):
+                engine.tensor_tensor(
+                    out=rotated[:, h0:h1], in0=terms[:, h0:h1, :, 0, :], in1=terms[:, h0:h1, :, 1, :], op=ALU.add
+                )
+                nc.sync.dma_start(
+                    out=out_rows[:, t, e0 + h0 * HEAD_DIM : e0 + h1 * HEAD_DIM],
+                    in_=rotated[:, h0:h1].rearrange("p h i o -> p (h i o)"),
+                )
 
         def build_rot(first_tile, n_tiles):
             tiles = slice(first_tile, first_tile + n_tiles)
@@ -329,12 +332,20 @@ def tile_flux2attention_pa_kernel(
                     load_rows("w", n + RAW_CHUNKS, tuple(range(CHUNK_ROW_TILES)))
 
         done = [0]
+        ended = set()
 
         def prepare(step):
             if step <= last:
                 wanted = max(done[0], pace(step))
-                to_quantise[step] = [transpose_unit(*unit) for unit in units[done[0] : wanted]]
+                to_quantise[step] = []
+                for i, unit in enumerate(units[done[0] : wanted]):
+                    if i == 1:
+                        at(norm_end, step - 1)
+                        ended.add(step - 1)
+                    to_quantise[step].append(transpose_unit(*unit))
                 done[0] = wanted
+            if step - 1 not in ended:
+                at(norm_end, step - 1)
 
         def finish(step):
             for piece in to_quantise.pop(step, ()):

import math
from contextlib import ExitStack

import concourse.mybir as mybir
from concourse.masks import make_identity

F32 = mybir.dt.float32
BF16 = mybir.dt.bfloat16
I32 = mybir.dt.int32
U32 = mybir.dt.uint32
U8 = mybir.dt.uint8
FP8X4 = mybir.dt.float8_e4m3fn_x4
ACT = mybir.ActivationFunctionType
ALU = mybir.AluOpType

P = 128
D_MODEL = 1536
WORDS = D_MODEL // 2
K_PASS = 512
PASSES = D_MODEL // K_PASS
HEAD_DIM = 128
PAIRS = HEAD_DIM // 2
E_OUT = 1536
CHUNK = 512
CHUNK_HEADS = CHUNK // HEAD_DIM
CHUNK_ROW_TILES = CHUNK // P
CHUNKS = E_OUT // CHUNK
TILES = 8
TEXT_TILES = 2
UNIT_ROW_TILES = 2
EPS = 1e-5
RAW_CHUNKS = 4
READY_STEPS = 2
READY_FIRST = 1
FIRST_STEPS = 2
UNITS_IN_A_RUN = 1
PARK_K_STEP = 33

FLOPS = 2 * 2 * 1024 * D_MODEL * E_OUT


def tile_flux2attention_pa_kernel(
    tc,
    hidden_states,
    encoder_hidden_states,
    rope_cos,
    rope_sin,
    Wq,
    Wk,
    Waq,
    baq,
    Wak,
    bak,
    wq_norm,
    wk_norm,
    waq_norm,
    wak_norm,
    out_0,
    out_1,
):
    nc = tc.nc
    with ExitStack() as ctx:
        ctx.enter_context(tc.manual_schedule())
        const = ctx.enter_context(tc.tile_pool(name="const", bufs=1))
        raw_pool = ctx.enter_context(tc.tile_pool(name="raw", bufs=RAW_CHUNKS))
        grouped_pool = ctx.enter_context(tc.tile_pool(name="grouped", bufs=8))
        quant_pool = ctx.enter_context(tc.tile_pool(name="quant", bufs=3))
        work = ctx.enter_context(tc.tile_pool(name="work", bufs=3))
        terms_pool = ctx.enter_context(tc.tile_pool(name="terms", bufs=5))
        rotated_pool = ctx.enter_context(tc.tile_pool(name="rotated", bufs=6))
        small = ctx.enter_context(tc.tile_pool(name="small", bufs=6))
        psum_t = ctx.enter_context(tc.psum_pool(name="psum_t", bufs=3))
        psum_acc = ctx.enter_context(tc.psum_pool(name="psum_acc", bufs=4))
        psum_f = ctx.enter_context(tc.psum_pool(name="psum_f", bufs=1))

        x_txt = encoder_hidden_states[0].rearrange("(t p) k -> p t k", p=P)
        x_img = hidden_states[0].rearrange("(t p) k -> p t k", p=P)
        out_q = out_0[0].rearrange("(t p) h d -> p t (h d)", p=P)
        out_k = out_1[0].rearrange("(t p) h d -> p t (h d)", p=P)

        x_raw = const.tile([P, TILES, D_MODEL], BF16)
        x_codes = const.tile([P, PASSES, TILES * P], U32, align_bytes=64)
        x_scales = const.tile([P, PASSES, TILES * P], U8, align_bytes=64)
        cos_sb = const.tile([P, TILES, HEAD_DIM], BF16)
        sin_sb = const.tile([P, TILES, HEAD_DIM], BF16)
        gain_rows = const.tile([P, 4 * HEAD_DIM], BF16)
        gain_sb = const.tile([P, 4, HEAD_DIM], BF16)
        bias_sb = const.tile([P, 2 * E_OUT], BF16)
        one = const.tile([P, 1], F32)
        unused = const.tile([P, 1], F32)
        ones = const.tile([P, P], BF16)
        ident = const.tile([P, P], F32)
        rot = const.tile([P, TILES, PAIRS, 2, 2], BF16)
        factors_q = {"sbuf": const.tile([P, TILES, HEAD_DIM, 2], F32, name="factors_q")}
        factors_k = {"sbuf": const.tile([P, TILES, HEAD_DIM, 2], F32, name="factors_k")}

        image_chunks, text_chunks, chunks = [], [], []
        for w_img, w_txt, bias_col, factors, out_rows in (
            (Wq, Waq, 0, factors_q, out_q),
            (Wk, Wak, E_OUT, factors_k, out_k),
        ):
            for c in range(CHUNKS):
                image_chunks.append((w_img, c * CHUNK, None, factors, out_rows, range(TEXT_TILES, TILES)))
                text_chunks.append((w_txt, c * CHUNK, bias_col + c * CHUNK, factors, out_rows, range(TEXT_TILES)))
        for i in range(2 * CHUNKS):
            chunks.append(image_chunks[i])
            if i > 0:
                chunks.append(text_chunks[i - 1])
        chunks.append(text_chunks[-1])
        works = [(n, t) for n in range(len(chunks)) for t in chunks[n][5]]

        first_tile = works[0][1]
        first_pieces = [("w", 0, (0,)), ("w", 0, (1,)), ("x", None, (first_tile,)), ("w", 0, (2,)), ("w", 0, (3,))]
        needs = []
        for n, t in works:
            pair = tuple(range(t - t % UNIT_ROW_TILES, t - t % UNIT_ROW_TILES + UNIT_ROW_TILES))
            for need in (("x", None, pair), ("w", n, tuple(range(CHUNK_ROW_TILES)))):
                if need[0] == "x":
                    need = ("x", None, tuple(tile for tile in pair if tile != first_tile))
                if need not in needs and need[1] != 0:
                    needs.append(need)
        first_units = [piece + (g,) for piece in first_pieces for g in range(PASSES)]
        units = []
        for kind, n, rows in needs:
            for g in range(PASSES):
                for i in range(0, len(rows), UNIT_ROW_TILES):
                    units.append((kind, n, rows[i : i + UNIT_ROW_TILES], g))

        w_raw = {}

        def load_rows(kind, n, rows):
            first, last = rows[0], rows[-1] + 1
            if kind == "x":
                stream, skip = (x_txt, 0) if first < TEXT_TILES else (x_img, TEXT_TILES)
                nc.sync.dma_start(out=x_raw[:, first:last, :], in_=stream[:, first - skip : last - skip, :])
                return
            weight, e0 = chunks[n][0], chunks[n][1]
            if n not in w_raw:
                w_raw[n] = raw_pool.tile([P, CHUNK_ROW_TILES, D_MODEL], BF16, name="w_raw")
            chunk_rows = weight[e0 : e0 + CHUNK, :].rearrange("(r p) k -> p r k", p=P)
            nc.sync.dma_start(out=w_raw[n][:, first:last, :], in_=chunk_rows[:, first:last, :])

        nc.vector.memset(gain_rows[:].bitcast(I32), 0)
        nc.vector.memset(ones[:], 1.0)
        nc.vector.memset(one[:], 1.0)
        make_identity(nc, ident[:])

        for i, gain in enumerate((wq_norm, wk_norm, waq_norm, wak_norm)):
            nc.scalar.dma_start(
                out=gain_rows[0:1, i * HEAD_DIM : (i + 1) * HEAD_DIM], in_=gain.rearrange("(o d) -> o d", o=1)
            )
        nc.scalar.activation(out=unused[:], in_=one[:], func=ACT.Abs_reciprocal_sqrt)
        for piece in first_pieces:
            load_rows(*piece)
        for i, (kind, n, rows) in enumerate(needs):
            if i == 1:
                for table_sb, table in ((cos_sb, rope_cos), (sin_sb, rope_sin)):
                    nc.sync.dma_start(out=table_sb[:], in_=table.rearrange("(t p) d -> p t d", p=P))
            if kind == "x" or n < RAW_CHUNKS:
                load_rows(kind, n, rows)
        for i, bias in enumerate((baq, bak)):
            nc.sync.dma_start(out=bias_sb[:, i * E_OUT : (i + 1) * E_OUT], in_=bias.partition_broadcast(P))

        def spread(rows, target):
            bank = psum_acc.tile([P, CHUNK], F32, name="acc")
            nc.tensor.matmul(out=bank[:], lhsT=ones[:], rhs=rows, start=True, stop=True)
            nc.scalar.copy(out=target, in_=bank[:])

        w_codes = {}
        w_scales = {}

        def transpose_unit(kind, n, rows, g, vector_copies=False):
            if kind == "x":
                words = x_raw[:].rearrange("p t k -> p (t k)").bitcast(F32)
                codes, scales = x_codes, x_scales
            else:
                if n not in w_codes:
                    w_codes[n] = quant_pool.tile([P, PASSES, CHUNK], U32, align_bytes=64, name="w_codes")
                    w_scales[n] = quant_pool.tile([P, PASSES, CHUNK], U8, align_bytes=64, name="w_scales")
                words = w_raw[n][:].rearrange("p r k -> p (r k)").bitcast(F32)
                codes, scales = w_codes[n], w_scales[n]
            n_rows = P * len(rows)
            xt = psum_t.tile([P, 2, n_rows], F32, name="xt")
            for u in range(2):
                for i, row_tile in enumerate(rows):
                    word = row_tile * WORDS + (K_PASS // 2) * g
                    nc.tensor.transpose(
                        xt[:, u, i * P : (i + 1) * P], words[:, word + u : word + K_PASS // 2 : 2], ident[:]
                    )
            grouped = grouped_pool.tile([P, 4 * n_rows], BF16, align_bytes=64, name="grouped")
            grouped_words = grouped[:].bitcast(F32).rearrange("p (c u) -> p c u", u=2)
            if vector_copies:
                nc.vector.tensor_copy(out=grouped_words, in_=xt[:].rearrange("p u c -> p c u"))
            else:
                nc.scalar.copy(out=grouped_words, in_=xt[:].rearrange("p u c -> p c u"))
            cols = slice(rows[0] * P, rows[0] * P + n_rows)
            return (grouped[:], codes[:, g, cols], scales[:, g, cols])

        def quantise(grouped, codes, scales):
            nc.vector.quantize_mx(out=codes.bitcast(FP8X4), scales=scales, in_=grouped)

        def multiply(n, t, state):
            state["acc"] = psum_acc.tile([P, CHUNK], F32, name="acc")
            for g in range(PASSES):
                nc.tensor.matmul_mx(
                    out=state["acc"][:],
                    lhsT=x_codes[:, g, t * P : (t + 1) * P].bitcast(FP8X4),
                    lhsT_scale=x_scales[:, g, t * P : (t + 1) * P],
                    rhs=w_codes[n][:, g, :].bitcast(FP8X4),
                    rhs_scale=w_scales[n][:, g, :],
                    start=(g == 0),
                    stop=(g == PASSES - 1),
                )

        def add_bias(n, t, state):
            bias_col = chunks[n][2]
            state["x"] = state["acc"]
            if bias_col is not None:
                state["x"] = work.tile([P, CHUNK], F32, name="biased")
                nc.vector.tensor_tensor(
                    out=state["x"][:], in0=state["acc"][:], in1=bias_sb[:, bias_col : bias_col + CHUNK], op=ALU.add
                )

        def norm(n, t, state):
            x = state["x"]
            squares = work.tile([P, CHUNK], BF16, name="squares")
            state["sum_sq"] = small.tile([P, CHUNK_HEADS], F32, name="sum_sq")
            for h in range(CHUNK_HEADS):
                head = slice(h * HEAD_DIM, (h + 1) * HEAD_DIM)
                nc.scalar.activation(
                    out=squares[:, head], in_=x[:, head], func=ACT.Square, accum_out=state["sum_sq"][:, h : h + 1]
                )
        def norm_end(n, t, state):
            state["r"] = small.tile([P, CHUNK_HEADS], F32, name="r")
            nc.scalar.activation(
                out=state["r"][:], in_=state["sum_sq"][:], func=ACT.Abs_reciprocal_sqrt, scale=1.0 / HEAD_DIM, bias=EPS
            )

        def rotate(n, t, state):
            factors = chunks[n][3]
            x, r = state["x"], state["r"]
            state["terms"] = terms_pool.tile([P, CHUNK_HEADS, PAIRS, 2, 2], F32, name="terms")
            for h in range(CHUNK_HEADS):
                nc.vector.scalar_tensor_tensor(
                    out=state["terms"][:, h].rearrange("p i j o -> p (i j) o"),
                    in0=x[:, h * HEAD_DIM : (h + 1) * HEAD_DIM].unsqueeze(2).to_broadcast([P, HEAD_DIM, 2]),
                    scalar=r[:, h : h + 1],
                    in1=factors["text" if t < TEXT_TILES else "sbuf"][:, t],
                    op0=ALU.mult,
                    op1=ALU.mult,
                )

        def add_and_store(n, t, state):
            e0, out_rows = chunks[n][1], chunks[n][4]
            terms = state["terms"]
            rotated = rotated_pool.tile([P, CHUNK_HEADS, PAIRS, 2], F32, name="rotated")
            halves = ((nc.gpsimd, 0, CHUNK_HEADS // 2), (nc.vector, CHUNK_HEADS // 2, CHUNK_HEADS))
            for engine, h0, h1 in halves if (n, t) == works[-1] else ((nc.gpsimd, 0, CHUNK_HEADS),):
                engine.tensor_tensor(
                    out=rotated[:, h0:h1], in0=terms[:, h0:h1, :, 0, :], in1=terms[:, h0:h1, :, 1, :], op=ALU.add
                )
                nc.sync.dma_start(
                    out=out_rows[:, t, e0 + h0 * HEAD_DIM : e0 + h1 * HEAD_DIM],
                    in_=rotated[:, h0:h1].rearrange("p h i o -> p (h i o)"),
                )

        def build_rot(first_tile, n_tiles):
            tiles = slice(first_tile, first_tile + n_tiles)
            cos = cos_sb[:, tiles].rearrange("p t (i o) -> p t i o", o=2)
            sin = sin_sb[:, tiles].rearrange("p t (i o) -> p t i o", o=2)
            nc.vector.tensor_copy(out=rot[:, tiles, :, 0, 0], in_=cos[:, :, :, 0])
            nc.vector.tensor_scalar_mul(out=rot[:, tiles, :, 1, 0], in0=sin[:, :, :, 0], scalar1=-1.0)
            nc.vector.tensor_copy(out=rot[:, tiles, :, 0, 1], in_=sin[:, :, :, 1])
            nc.vector.tensor_copy(out=rot[:, tiles, :, 1, 1], in_=cos[:, :, :, 1])

        def build_factors(factors, first_tile, n_tiles, gain_index, engine):
            tiles = slice(first_tile, first_tile + n_tiles)
            engine.tensor_tensor(
                out=factors["sbuf"][:, tiles],
                in0=rot[:, tiles].rearrange("p t i j o -> p t (i j) o"),
                in1=gain_sb[:, gain_index : gain_index + 1, :].unsqueeze(3).to_broadcast([P, n_tiles, HEAD_DIM, 2]),
                op=ALU.mult,
            )

        def park_text_factors(factors):
            factors["text"] = psum_f.tile([P, TEXT_TILES, HEAD_DIM, 2], F32, name="text_factors")
            nc.tensor.matmul(
                out=factors["text"][:].rearrange("p t d o -> p (t d o)"),
                lhsT=ident[:],
                rhs=factors["sbuf"][:, 0:TEXT_TILES].rearrange("p t d o -> p (t d o)"),
                start=True,
                stop=True,
            )

        for unit in first_units:
            quantise(*transpose_unit(*unit))
        spread(gain_rows[:], gain_sb[:].rearrange("p i d -> p (i d)"))
        build_rot(TEXT_TILES, TILES - TEXT_TILES)
        build_factors(factors_q, TEXT_TILES, 1, 0, nc.vector)

        due = []
        for step in range(len(works)):
            ready = READY_FIRST if step < FIRST_STEPS else READY_STEPS
            tiles_and_chunks = works[: step + 1 + ready]
            due.append(
                sum(
                    any((kind == "w" and n == unit_n) or (kind == "x" and t in rows) for n, t in tiles_and_chunks)
                    for kind, unit_n, rows, g in units
                )
            )

        def pace(step):
            known = [(-1, 0)] + list(enumerate(due))
            hull = max(
                ya + (yb - ya) * (step - a) / (b - a) for a, ya in known for b, yb in known if a < step <= b
            )
            return UNITS_IN_A_RUN * math.ceil((hull - 1e-9) / UNITS_IN_A_RUN)

        prepared = 0
        states = {}
        to_quantise = {}
        last = len(works) - 1

        def at(stage, s):
            if 0 <= s <= last:
                stage(works[s][0], works[s][1], states[s])

        def start_chunk(step):
            n, t = works[step]
            if step == 0 or works[step - 1][0] != n:
                if n + RAW_CHUNKS < len(chunks):
                    load_rows("w", n + RAW_CHUNKS, tuple(range(CHUNK_ROW_TILES)))

        done = [0]
        ended = set()

        def prepare(step):
            if step <= last:
                wanted = max(done[0], pace(step))
                to_quantise[step] = []
                for i, unit in enumerate(units[done[0] : wanted]):
                    if i == 1:
                        at(norm_end, step - 1)
                        ended.add(step - 1)
                    to_quantise[step].append(transpose_unit(*unit))
                done[0] = wanted
            if step - 1 not in ended:
                at(norm_end, step - 1)

        def finish(step):
            for piece in to_quantise.pop(step, ()):
                quantise(*piece)

        def tables(step):
            if step + TEXT_TILES + 1 < TILES:
                build_factors(factors_q, step + TEXT_TILES + 1, 1, 0, nc.vector)
            if step == 2:
                build_rot(0, TEXT_TILES)
                build_factors(factors_q, 0, TEXT_TILES, 2, nc.vector)
            if step in (4, 5, 6):
                build_factors(factors_k, 2 * step - 6, 2, 1, nc.gpsimd)
            if step == 7:
                build_factors(factors_k, 0, TEXT_TILES, 3, nc.gpsimd)
            if step == 5:
                park_text_factors(factors_q)
            if step == PARK_K_STEP:
                park_text_factors(factors_k)

        for step in range(len(works) + 1):
            if step <= last:
                states[step] = {}
                start_chunk(step)
            prepare(step)
            at(multiply, step)
            at(add_bias, step)
            at(norm, step)
            at(rotate, step - 1)
            at(add_and_store, step - 1)
            finish(step)
            tables(step)
